import numpy as np
import ml_dtypes


def mxq(x, axis, fmt="e4m3"):
    dtype, down = {"e4m3": (ml_dtypes.float8_e4m3fn, 7), "e5m2": (ml_dtypes.float8_e5m2, 14)}[fmt]
    v = np.moveaxis(np.asarray(x, np.float32).astype(ml_dtypes.bfloat16).astype(np.float64), axis, -1)
    blocks = v.reshape(v.shape[:-1] + (-1, 32))
    amax = np.abs(blocks).max(-1, keepdims=True)
    byte = np.maximum(np.where(amax > 0, np.frexp(amax)[1] - 1 + 127, 0) - down, 1)
    scale = np.exp2(byte - 127.0)
    codes = (blocks / scale).astype(np.float32).astype(dtype).astype(np.float64)
    return np.moveaxis((codes * scale).reshape(v.shape), -1, axis)


WIDE = False


def mx_kscale(k):
    if not WIDE:
        return np.ones(k)
    levels = np.array([20, -20, 10, -10, 0])
    a = np.random.permutation(np.resize(levels, k // 512 * 4)).reshape(k // 512, 4)
    idx = np.arange(k)
    return np.exp2(a[idx // 512, idx % 128 // 32])


BF16 = ml_dtypes.bfloat16


def bf(x):
    return np.asarray(x, np.float32).astype(BF16)


def f64(x):
    return np.asarray(x).astype(np.float64)


B, S, HID, NH, NOPE, ROPE, VD, KV_RANK, SW, QB = 1, 512, 512, 8, 64, 64, 128, 512, 384, 128
QK = NOPE + ROPE


def rotate_half(x):
    h = x.shape[-1] // 2
    return np.concatenate([-x[..., h:], x[..., :h]], axis=-1)


def rotate_half_t(y):
    h = y.shape[-1] // 2
    return np.concatenate([y[..., h:], -y[..., :h]], axis=-1)


def rope_tables():
    pos = np.arange(S, dtype=np.float64)
    inv = 1.0 / (10000.0 ** (np.arange(0, ROPE, 2, dtype=np.float64) / ROPE))
    ang = pos[:, None] * inv[None, :]
    ang = np.concatenate([ang, ang], axis=-1)
    return bf(np.broadcast_to(np.cos(ang)[None], (B, S, ROPE))), bf(np.broadcast_to(np.sin(ang)[None], (B, S, ROPE)))


def setup_inputs():
    u = np.array(mx_kscale(NH * QK), dtype=np.float64).reshape(NH, QK)
    u[:, NOPE + ROPE // 2:] = u[:, NOPE:NOPE + ROPE // 2]
    cos, sin = rope_tables()
    hs = np.random.standard_normal((B, S, HID))
    wq = np.random.standard_normal((HID, NH * QK)) * 2.0 / np.sqrt(HID) / u.reshape(-1)[None, :]
    b = np.random.standard_normal(NH * QK) * 0.2
    g = np.random.standard_normal((B, NH, S, QK)) * np.exp2(np.random.randint(-12, 1, (B, 1, S, 1))) * 4.0 * u[None, :, None, :]
    return {"hidden_states": bf(hs), "cos": cos, "sin": sin, "Wq": bf(wq), "bq": bf(b), "grad_out": bf(g)}


def reference(hidden_states, cos, sin, Wq, bq, grad_out):
    g = f64(grad_out)
    c, si = f64(cos)[:, None], f64(sin)[:, None]
    g_nope, g_rope = g[..., :NOPE], g[..., NOPE:]
    gq_rope = g_rope * c + rotate_half_t(g_rope * si)
    gq = np.concatenate([g_nope, gq_rope], axis=-1).transpose(0, 2, 1, 3).reshape(B, S, NH * QK)
    return mxq(gq, 2, "e5m2") @ mxq(f64(Wq), 1, "e4m3").T

@@ -1,0 +1,153 @@
+from contextlib import ExitStack
+
+import concourse.mybir as mybir
+from concourse.masks import make_identity
+
+BF16 = mybir.dt.bfloat16
+F32 = mybir.dt.float32
+U32 = mybir.dt.uint32
+U8 = mybir.dt.uint8
+E4M3_X4 = mybir.dt.float8_e4m3fn_x4
+E5M2_X4 = mybir.dt.float8_e5m2_x4
+
+P = 128
+SEQ = 512
+HID = 512
+HEADS = 8
+HEAD_DIM = 128
+NOPE = 64
+ROPE = 64
+HALF = ROPE // 2
+K = HEADS * HEAD_DIM
+K_PASS = 4 * P
+PASSES = K // K_PASS
+S_TILES = SEQ // P
+I_TILES = HID // P
+PAIRS_PER_PASS = K_PASS // 2
+
+FLOPS = 2 * SEQ * HID * K
+BYTES = 2 * (2 * SEQ * ROPE + HID * K + SEQ * K) + 4 * SEQ * HID
+
+
+def tile_gptossmlaattention_pb_s_kernel(tc, hidden_states, cos, sin, Wq, bq, grad_out, out):
+    nc = tc.nc
+    with ExitStack() as ctx:
+        keep = ctx.enter_context(tc.tile_pool(name="keep", bufs=1))
+        scratch = ctx.enter_context(tc.tile_pool(name="scratch", bufs=2))
+        flip_banks = ctx.enter_context(tc.psum_pool(name="flip_banks", bufs=4))
+        sum_banks = ctx.enter_context(tc.psum_pool(name="sum_banks", bufs=1))
+
+        cos_sb = keep.tile([P, S_TILES, ROPE], BF16, name="cos_sb")
+        sin_sb = keep.tile([P, S_TILES, ROPE], BF16, name="sin_sb")
+        g_sb = [keep.tile([P, HEADS, HEAD_DIM], BF16, name="g_sb%d" % r) for r in range(S_TILES)]
+        w_sb = [keep.tile([P, I_TILES, K_PASS], BF16, name="w_sb%d" % c) for c in range(PASSES)]
+        g_dram = grad_out.rearrange("b h (p r) d -> r p (b h) d", r=S_TILES)
+        w_dram = Wq.rearrange("(a p) (c k) -> c p a k", p=P, c=PASSES)
+
+        nc.sync.dma_start(out=cos_sb[:], in_=cos.rearrange("b (p r) j -> p (b r) j", r=S_TILES))
+        nc.sync.dma_start(out=sin_sb[:], in_=sin.rearrange("b (p r) j -> p (b r) j", r=S_TILES))
+        nc.sync.dma_start(out=g_sb[0][:], in_=g_dram[0])
+        nc.sync.dma_start(out=g_sb[1][:], in_=g_dram[1])
+        nc.sync.dma_start(out=w_sb[0][:], in_=w_dram[0])
+        nc.sync.dma_start(out=g_sb[2][:], in_=g_dram[2])
+        nc.sync.dma_start(out=w_sb[1][:], in_=w_dram[1])
+        nc.sync.dma_start(out=g_sb[3][:], in_=g_dram[3])
+
+        ident = keep.tile([P, P], F32, name="ident")
+        make_identity(nc, ident[:])
+
+        factors = keep.tile([P, S_TILES, 2, ROPE], BF16, name="factors")
+        nc.vector.tensor_copy(out=factors[:, :, 0, 0:HALF], in_=cos_sb[:, :, 0:HALF])
+        nc.vector.tensor_copy(out=factors[:, :, 0, HALF:ROPE], in_=sin_sb[:, :, HALF:ROPE])
+        nc.vector.tensor_scalar_mul(out=factors[:, :, 1, 0:HALF], in0=sin_sb[:, :, 0:HALF], scalar1=-1.0)
+        nc.vector.tensor_copy(out=factors[:, :, 1, HALF:ROPE], in_=cos_sb[:, :, HALF:ROPE])
+
+        g_words = [keep.tile([P, PASSES, P, 2], F32, name="g_words%d" % r, align_bytes=64) for r in range(S_TILES)]
+        g_codes = [keep.tile([P, PASSES, P], U32, name="g_codes%d" % r, align_bytes=64) for r in range(S_TILES)]
+        g_scales = [keep.tile([P, PASSES, P], U8, name="g_scales%d" % r, align_bytes=64) for r in range(S_TILES)]
+        w_words = [keep.tile([P, I_TILES, P, 2], F32, name="w_words%d" % c, align_bytes=64) for c in range(PASSES)]
+        w_codes = [keep.tile([P, HID], U32, name="w_codes%d" % c, align_bytes=64) for c in range(PASSES)]
+        w_scales = [keep.tile([P, HID], U8, name="w_scales%d" % c, align_bytes=64) for c in range(PASSES)]
+        sums = [sum_banks.tile([P, HID], F32, name="sums%d" % r) for r in range(S_TILES)]
+        result = [keep.tile([P, HID], F32, name="result%d" % r) for r in range(S_TILES)]
+        out_dram = out.rearrange("b (p r) i -> p (b r) i", r=S_TILES)
+
+        def undo_rotation(r):
+            rotated = g_sb[r][:, :, NOPE:HEAD_DIM]
+            products = scratch.tile([P, HEADS, 2, ROPE], F32, name="products")
+            nc.vector.tensor_mul(
+                out=products[:],
+                in0=rotated.unsqueeze(2).to_broadcast([P, HEADS, 2, ROPE]),
+                in1=factors[:, r].unsqueeze(1).to_broadcast([P, HEADS, 2, ROPE]),
+            )
+            nc.vector.tensor_add(
+                out=rotated.rearrange("p h (w j) -> p h w j", w=2),
+                in0=products[:, :, :, 0:HALF],
+                in1=products[:, :, :, HALF:ROPE],
+            )
+
+        def k_onto_partitions(blocks, words):
+            flipped = flip_banks.tile([P, 2, 2, P], F32, name="flipped")
+            for x in range(2):
+                for u in range(2):
+                    nc.tensor.transpose(flipped[:, x, u, :], blocks[x][:, u * P : (u + 1) * P], ident[:])
+            nc.scalar.copy(out=words, in_=flipped[:].rearrange("q x u n -> q x n u"))
+
+        def regroup_g(r):
+            pairs = g_sb[r][:].rearrange("p h d -> p (h d)").bitcast(F32)
+            blocks = [pairs[:, c * PAIRS_PER_PASS : (c + 1) * PAIRS_PER_PASS] for c in range(PASSES)]
+            k_onto_partitions(blocks, g_words[r][:])
+
+        def regroup_w(c):
+            for a in range(0, I_TILES, 2):
+                blocks = [w_sb[c][:, a + x, :].bitcast(F32) for x in range(2)]
+                k_onto_partitions(blocks, w_words[c][:, a : a + 2])
+
+        def quantise_g(r):
+            nc.vector.quantize_mx(
+                out=g_codes[r][:].rearrange("q c n -> q (c n)").bitcast(E5M2_X4),
+                scales=g_scales[r][:].rearrange("q c n -> q (c n)"),
+                in_=g_words[r][:].rearrange("q c n u -> q (c n u)").bitcast(BF16),
+            )
+
+        def quantise_w(c):
+            nc.vector.quantize_mx(
+                out=w_codes[c][:].bitcast(E4M3_X4),
+                scales=w_scales[c][:],
+                in_=w_words[c][:].rearrange("q a n u -> q (a n u)").bitcast(BF16),
+            )
+
+        def multiply(r, c):
+            nc.tensor.matmul_mx(
+                out=sums[r][:],
+                lhsT=g_codes[r][:, c, :].bitcast(E5M2_X4),
+                lhsT_scale=g_scales[r][:, c, :],
+                rhs=w_codes[c][:].bitcast(E4M3_X4),
+                rhs_scale=w_scales[c][:],
+                start=(c == 0),
+                stop=(c == PASSES - 1),
+            )
+
+        def store(r):
+            if r % 2 == 0:
+                nc.scalar.copy(out=result[r][:], in_=sums[r][:])
+            else:
+                nc.vector.tensor_copy(out=result[r][:], in_=sums[r][:])
+            nc.sync.dma_start(out=out_dram[:, r, :], in_=result[r][:])
+
+        for step in range(S_TILES + 1):
+            if step < S_TILES:
+                undo_rotation(step)
+                regroup_g(step)
+            if 1 <= step <= PASSES:
+                regroup_w(step - 1)
+            if step >= 1:
+                quantise_g(step - 1)
+            if 2 <= step <= PASSES + 1:
+                quantise_w(step - 2)
+            for c in range(PASSES):
+                for r in range(S_TILES):
+                    if max(r + 1, c + 2) == step:
+                        multiply(r, c)
+        for r in range(S_TILES):
+            store(r)

@@ -36,6 +36,7 @@ def tile_gptossmlaattention_pb_s_kernel(tc, hidden_states, cos, sin, Wq, bq, gra
         scratch = ctx.enter_context(tc.tile_pool(name="scratch", bufs=2))
         flip_banks = ctx.enter_context(tc.psum_pool(name="flip_banks", bufs=4))
         sum_banks = ctx.enter_context(tc.psum_pool(name="sum_banks", bufs=1))
+        ctx.enter_context(tc.manual_schedule())
 
         cos_sb = keep.tile([P, S_TILES, ROPE], BF16, name="cos_sb")
         sin_sb = keep.tile([P, S_TILES, ROPE], BF16, name="sin_sb")

@@ -23,7 +23,11 @@ K_PASS = 4 * P
 PASSES = K // K_PASS
 S_TILES = SEQ // P
 I_TILES = HID // P
-PAIRS_PER_PASS = K_PASS // 2
+HEADS_PER_PASS = K_PASS // HEAD_DIM
+UNITS = S_TILES * PASSES
+W_BLOCKS = PASSES * I_TILES
+LAG = 3
+W_FIRST = 3
 
 FLOPS = 2 * SEQ * HID * K
 BYTES = 2 * (2 * SEQ * ROPE + HID * K + SEQ * K) + 4 * SEQ * HID
@@ -33,26 +37,31 @@ def tile_gptossmlaattention_pb_s_kernel(tc, hidden_states, cos, sin, Wq, bq, gra
     nc = tc.nc
     with ExitStack() as ctx:
         keep = ctx.enter_context(tc.tile_pool(name="keep", bufs=1))
-        scratch = ctx.enter_context(tc.tile_pool(name="scratch", bufs=2))
+        scratch = ctx.enter_context(tc.tile_pool(name="scratch", bufs=3))
         flip_banks = ctx.enter_context(tc.psum_pool(name="flip_banks", bufs=4))
         sum_banks = ctx.enter_context(tc.psum_pool(name="sum_banks", bufs=1))
         ctx.enter_context(tc.manual_schedule())
 
         cos_sb = keep.tile([P, S_TILES, ROPE], BF16, name="cos_sb")
         sin_sb = keep.tile([P, S_TILES, ROPE], BF16, name="sin_sb")
-        g_sb = [keep.tile([P, HEADS, HEAD_DIM], BF16, name="g_sb%d" % r) for r in range(S_TILES)]
+        g_sb = [keep.tile([P, HEADS_PER_PASS, HEAD_DIM], BF16, name="g_sb%d" % j) for j in range(UNITS)]
         w_sb = [keep.tile([P, I_TILES, K_PASS], BF16, name="w_sb%d" % c) for c in range(PASSES)]
-        g_dram = grad_out.rearrange("b h (p r) d -> r p (b h) d", r=S_TILES)
+        g_dram = grad_out.rearrange("b (c h) (p r) d -> r c p (b h) d", c=PASSES, r=S_TILES)
         w_dram = Wq.rearrange("(a p) (c k) -> c p a k", p=P, c=PASSES)
+
+        def load_g(j):
+            nc.sync.dma_start(out=g_sb[j][:], in_=g_dram[j // PASSES, j % PASSES])
 
         nc.sync.dma_start(out=cos_sb[:], in_=cos.rearrange("b (p r) j -> p (b r) j", r=S_TILES))
         nc.sync.dma_start(out=sin_sb[:], in_=sin.rearrange("b (p r) j -> p (b r) j", r=S_TILES))
-        nc.sync.dma_start(out=g_sb[0][:], in_=g_dram[0])
-        nc.sync.dma_start(out=g_sb[1][:], in_=g_dram[1])
+        for j in range(0, 4):
+            load_g(j)
         nc.sync.dma_start(out=w_sb[0][:], in_=w_dram[0])
-        nc.sync.dma_start(out=g_sb[2][:], in_=g_dram[2])
+        for j in range(4, 6):
+            load_g(j)
         nc.sync.dma_start(out=w_sb[1][:], in_=w_dram[1])
-        nc.sync.dma_start(out=g_sb[3][:], in_=g_dram[3])
+        for j in range(6, 8):
+            load_g(j)
 
         ident = keep.tile([P, P], F32, name="ident")
         make_identity(nc, ident[:])
@@ -63,52 +72,43 @@ def tile_gptossmlaattention_pb_s_kernel(tc, hidden_states, cos, sin, Wq, bq, gra
         nc.vector.tensor_scalar_mul(out=factors[:, :, 1, 0:HALF], in0=sin_sb[:, :, 0:HALF], scalar1=-1.0)
         nc.vector.tensor_copy(out=factors[:, :, 1, HALF:ROPE], in_=cos_sb[:, :, HALF:ROPE])
 
-        g_words = [keep.tile([P, PASSES, P, 2], F32, name="g_words%d" % r, align_bytes=64) for r in range(S_TILES)]
-        g_codes = [keep.tile([P, PASSES, P], U32, name="g_codes%d" % r, align_bytes=64) for r in range(S_TILES)]
-        g_scales = [keep.tile([P, PASSES, P], U8, name="g_scales%d" % r, align_bytes=64) for r in range(S_TILES)]
+        g_words = [keep.tile([P, P, 2], F32, name="g_words%d" % j, align_bytes=64) for j in range(UNITS)]
+        g_codes = [keep.tile([P, P], U32, name="g_codes%d" % j, align_bytes=64) for j in range(UNITS)]
+        g_scales = [keep.tile([P, P], U8, name="g_scales%d" % j, align_bytes=64) for j in range(UNITS)]
         w_words = [keep.tile([P, I_TILES, P, 2], F32, name="w_words%d" % c, align_bytes=64) for c in range(PASSES)]
         w_codes = [keep.tile([P, HID], U32, name="w_codes%d" % c, align_bytes=64) for c in range(PASSES)]
         w_scales = [keep.tile([P, HID], U8, name="w_scales%d" % c, align_bytes=64) for c in range(PASSES)]
         sums = [sum_banks.tile([P, HID], F32, name="sums%d" % r) for r in range(S_TILES)]
         result = [keep.tile([P, HID], F32, name="result%d" % r) for r in range(S_TILES)]
         out_dram = out.rearrange("b (p r) i -> p (b r) i", r=S_TILES)
+        products = {}
 
-        def undo_rotation(r):
-            rotated = g_sb[r][:, :, NOPE:HEAD_DIM]
-            products = scratch.tile([P, HEADS, 2, ROPE], F32, name="products")
+        def multiply_by_factors(j):
+            products[j] = scratch.tile([P, HEADS_PER_PASS, 2, ROPE], F32, name="products")
             nc.vector.tensor_mul(
-                out=products[:],
-                in0=rotated.unsqueeze(2).to_broadcast([P, HEADS, 2, ROPE]),
-                in1=factors[:, r].unsqueeze(1).to_broadcast([P, HEADS, 2, ROPE]),
+                out=products[j][:],
+                in0=g_sb[j][:, :, NOPE:HEAD_DIM].unsqueeze(2).to_broadcast([P, HEADS_PER_PASS, 2, ROPE]),
+                in1=factors[:, j // PASSES].unsqueeze(1).to_broadcast([P, HEADS_PER_PASS, 2, ROPE]),
             )
+
+        def add_products(j):
             nc.vector.tensor_add(
-                out=rotated.rearrange("p h (w j) -> p h w j", w=2),
-                in0=products[:, :, :, 0:HALF],
-                in1=products[:, :, :, HALF:ROPE],
+                out=g_sb[j][:, :, NOPE:HEAD_DIM].rearrange("p h (w j) -> p h w j", w=2),
+                in0=products[j][:, :, :, 0:HALF],
+                in1=products[j][:, :, :, HALF:ROPE],
             )
 
-        def k_onto_partitions(blocks, words):
-            flipped = flip_banks.tile([P, 2, 2, P], F32, name="flipped")
-            for x in range(2):
-                for u in range(2):
-                    nc.tensor.transpose(flipped[:, x, u, :], blocks[x][:, u * P : (u + 1) * P], ident[:])
-            nc.scalar.copy(out=words, in_=flipped[:].rearrange("q x u n -> q x n u"))
+        def k_onto_partitions(block, words):
+            flipped = flip_banks.tile([P, 2, P], F32, name="flipped")
+            for u in range(2):
+                nc.tensor.transpose(flipped[:, u, :], block[:, u * P : (u + 1) * P], ident[:])
+            nc.scalar.copy(out=words, in_=flipped[:].rearrange("q u n -> q n u"))
 
-        def regroup_g(r):
-            pairs = g_sb[r][:].rearrange("p h d -> p (h d)").bitcast(F32)
-            blocks = [pairs[:, c * PAIRS_PER_PASS : (c + 1) * PAIRS_PER_PASS] for c in range(PASSES)]
-            k_onto_partitions(blocks, g_words[r][:])
-
-        def regroup_w(c):
-            for a in range(0, I_TILES, 2):
-                blocks = [w_sb[c][:, a + x, :].bitcast(F32) for x in range(2)]
-                k_onto_partitions(blocks, w_words[c][:, a : a + 2])
-
-        def quantise_g(r):
+        def quantise_g(j):
             nc.vector.quantize_mx(
-                out=g_codes[r][:].rearrange("q c n -> q (c n)").bitcast(E5M2_X4),
-                scales=g_scales[r][:].rearrange("q c n -> q (c n)"),
-                in_=g_words[r][:].rearrange("q c n u -> q (c n u)").bitcast(BF16),
+                out=g_codes[j][:].bitcast(E5M2_X4),
+                scales=g_scales[j][:],
+                in_=g_words[j][:].rearrange("q n u -> q (n u)").bitcast(BF16),
             )
 
         def quantise_w(c):
@@ -121,8 +121,8 @@ def tile_gptossmlaattention_pb_s_kernel(tc, hidden_states, cos, sin, Wq, bq, gra
         def multiply(r, c):
             nc.tensor.matmul_mx(
                 out=sums[r][:],
-                lhsT=g_codes[r][:, c, :].bitcast(E5M2_X4),
-                lhsT_scale=g_scales[r][:, c, :],
+                lhsT=g_codes[r * PASSES + c][:].bitcast(E5M2_X4),
+                lhsT_scale=g_scales[r * PASSES + c][:],
                 rhs=w_codes[c][:].bitcast(E4M3_X4),
                 rhs_scale=w_scales[c][:],
                 start=(c == 0),
@@ -136,19 +136,27 @@ def tile_gptossmlaattention_pb_s_kernel(tc, hidden_states, cos, sin, Wq, bq, gra
                 nc.vector.tensor_copy(out=result[r][:], in_=sums[r][:])
             nc.sync.dma_start(out=out_dram[:, r, :], in_=result[r][:])
 
-        for step in range(S_TILES + 1):
-            if step < S_TILES:
-                undo_rotation(step)
-                regroup_g(step)
-            if 1 <= step <= PASSES:
-                regroup_w(step - 1)
-            if step >= 1:
-                quantise_g(step - 1)
-            if 2 <= step <= PASSES + 1:
-                quantise_w(step - 2)
+        def step_of_quantise_w(c):
+            return W_FIRST + 2 * c + 3
+
+        for step in range(UNITS + LAG):
+            if step < UNITS:
+                multiply_by_factors(step)
+            if 1 <= step <= UNITS:
+                add_products(step - 1)
+                k_onto_partitions(g_sb[step - 1][:].rearrange("p h d -> p (h d)").bitcast(F32), g_words[step - 1][:])
+            for b in range(2 * (step - W_FIRST), 2 * (step - W_FIRST) + 2):
+                if 0 <= b < W_BLOCKS:
+                    c, a = divmod(b, I_TILES)
+                    k_onto_partitions(w_sb[c][:, a, :].bitcast(F32), w_words[c][:, a])
+            if step >= LAG:
+                quantise_g(step - LAG)
+            for c in range(PASSES):
+                if step == step_of_quantise_w(c):
+                    quantise_w(c)
             for c in range(PASSES):
                 for r in range(S_TILES):
-                    if max(r + 1, c + 2) == step:
+                    if max(r * PASSES + c + LAG, step_of_quantise_w(c)) == step:
                         multiply(r, c)
         for r in range(S_TILES):
             store(r)

@@ -25,9 +25,8 @@ S_TILES = SEQ // P
 I_TILES = HID // P
 HEADS_PER_PASS = K_PASS // HEAD_DIM
 UNITS = S_TILES * PASSES
-W_BLOCKS = PASSES * I_TILES
-LAG = 3
-W_FIRST = 3
+HALVES = 2 * PASSES
+S_PAIRS = S_TILES // 2
 
 FLOPS = 2 * SEQ * HID * K
 BYTES = 2 * (2 * SEQ * ROPE + HID * K + SEQ * K) + 4 * SEQ * HID
@@ -37,92 +36,127 @@ def tile_gptossmlaattention_pb_s_kernel(tc, hidden_states, cos, sin, Wq, bq, gra
     nc = tc.nc
     with ExitStack() as ctx:
         keep = ctx.enter_context(tc.tile_pool(name="keep", bufs=1))
-        scratch = ctx.enter_context(tc.tile_pool(name="scratch", bufs=3))
-        flip_banks = ctx.enter_context(tc.psum_pool(name="flip_banks", bufs=4))
-        sum_banks = ctx.enter_context(tc.psum_pool(name="sum_banks", bufs=1))
+        scratch = ctx.enter_context(tc.tile_pool(name="scratch", bufs=5))
+        flip_banks = ctx.enter_context(tc.psum_pool(name="flip_banks", bufs=5))
+        sum_banks = ctx.enter_context(tc.psum_pool(name="sum_banks", bufs=3))
         ctx.enter_context(tc.manual_schedule())
 
         cos_sb = keep.tile([P, S_TILES, ROPE], BF16, name="cos_sb")
         sin_sb = keep.tile([P, S_TILES, ROPE], BF16, name="sin_sb")
-        g_sb = [keep.tile([P, HEADS_PER_PASS, HEAD_DIM], BF16, name="g_sb%d" % j) for j in range(UNITS)]
-        w_sb = [keep.tile([P, I_TILES, K_PASS], BF16, name="w_sb%d" % c) for c in range(PASSES)]
-        g_dram = grad_out.rearrange("b (c h) (p r) d -> r c p (b h) d", c=PASSES, r=S_TILES)
-        w_dram = Wq.rearrange("(a p) (c k) -> c p a k", p=P, c=PASSES)
+        raw = [
+            [keep.tile([P, HEADS_PER_PASS, 2, HEAD_DIM], BF16, name="raw%d%d" % (R, c)) for c in range(PASSES)]
+            for R in range(S_PAIRS)
+        ]
+        w_sb = [keep.tile([P, K], BF16, name="w_sb%d" % a) for a in range(I_TILES)]
+        g_dram = grad_out.rearrange("b (c h) (R p e) d -> R c p (b h) (e d)", c=PASSES, R=S_PAIRS, e=2)
+        w_dram = Wq.rearrange("(a p) k -> a p k", p=P)
 
-        def load_g(j):
-            nc.sync.dma_start(out=g_sb[j][:], in_=g_dram[j // PASSES, j % PASSES])
+        def load_g(R, c):
+            nc.sync.dma_start(out=raw[R][c][:].rearrange("p h e d -> p h (e d)"), in_=g_dram[R, c])
 
-        nc.sync.dma_start(out=cos_sb[:], in_=cos.rearrange("b (p r) j -> p (b r) j", r=S_TILES))
-        nc.sync.dma_start(out=sin_sb[:], in_=sin.rearrange("b (p r) j -> p (b r) j", r=S_TILES))
-        for j in range(0, 4):
-            load_g(j)
-        nc.sync.dma_start(out=w_sb[0][:], in_=w_dram[0])
-        for j in range(4, 6):
-            load_g(j)
-        nc.sync.dma_start(out=w_sb[1][:], in_=w_dram[1])
-        for j in range(6, 8):
-            load_g(j)
+        def load_w(a):
+            nc.sync.dma_start(out=w_sb[a][:], in_=w_dram[a])
+
+        def load_table(tile, table):
+            nc.sync.dma_start(
+                out=tile[:].rearrange("p (R e) j -> p R (e j)", e=2),
+                in_=table.rearrange("b (R p e) j -> p (b R) (e j)", R=S_PAIRS, e=2),
+            )
+
+        load_table(cos_sb, cos)
+        load_table(sin_sb, sin)
+        for j in range(4):
+            load_g(j // PASSES, j % PASSES)
+            load_w(j)
 
         ident = keep.tile([P, P], F32, name="ident")
         make_identity(nc, ident[:])
 
-        factors = keep.tile([P, S_TILES, 2, ROPE], BF16, name="factors")
-        nc.vector.tensor_copy(out=factors[:, :, 0, 0:HALF], in_=cos_sb[:, :, 0:HALF])
-        nc.vector.tensor_copy(out=factors[:, :, 0, HALF:ROPE], in_=sin_sb[:, :, HALF:ROPE])
-        nc.vector.tensor_scalar_mul(out=factors[:, :, 1, 0:HALF], in0=sin_sb[:, :, 0:HALF], scalar1=-1.0)
-        nc.vector.tensor_copy(out=factors[:, :, 1, HALF:ROPE], in_=cos_sb[:, :, HALF:ROPE])
+        plus = keep.tile([P, P], BF16, name="plus")
+        minus = keep.tile([P, P], BF16, name="minus")
+        nc.vector.tensor_copy(out=plus[:], in_=ident[:])
+        nc.vector.tensor_scalar_mul(out=minus[:], in0=ident[:], scalar1=-1.0)
+        factors = sum_banks.tile([P, S_TILES, 2, ROPE], F32, name="sums")
+        for w, half, sign, table in ((0, 0, plus, cos_sb), (0, 1, plus, sin_sb), (1, 0, minus, sin_sb), (1, 1, plus, cos_sb)):
+            part = slice(half * HALF, (half + 1) * HALF)
+            nc.tensor.matmul(factors[:, :, w, part], lhsT=sign[:], rhs=table[:, :, part], start=True, stop=True)
 
-        g_words = [keep.tile([P, P, 2], F32, name="g_words%d" % j, align_bytes=64) for j in range(UNITS)]
-        g_codes = [keep.tile([P, P], U32, name="g_codes%d" % j, align_bytes=64) for j in range(UNITS)]
-        g_scales = [keep.tile([P, P], U8, name="g_scales%d" % j, align_bytes=64) for j in range(UNITS)]
-        w_words = [keep.tile([P, I_TILES, P, 2], F32, name="w_words%d" % c, align_bytes=64) for c in range(PASSES)]
+        g_words = [keep.tile([P, PASSES, P, 2], F32, name="g_words%d" % r, align_bytes=64) for r in range(S_TILES)]
+        g_codes = [keep.tile([P, PASSES, P], U32, name="g_codes%d" % r, align_bytes=64) for r in range(S_TILES)]
+        g_scales = [keep.tile([P, PASSES, P], U8, name="g_scales%d" % r, align_bytes=64) for r in range(S_TILES)]
+        w_words = keep.tile([P, PASSES, I_TILES, P, 2], F32, name="w_words", align_bytes=64)
         w_codes = [keep.tile([P, HID], U32, name="w_codes%d" % c, align_bytes=64) for c in range(PASSES)]
         w_scales = [keep.tile([P, HID], U8, name="w_scales%d" % c, align_bytes=64) for c in range(PASSES)]
-        sums = [sum_banks.tile([P, HID], F32, name="sums%d" % r) for r in range(S_TILES)]
         result = [keep.tile([P, HID], F32, name="result%d" % r) for r in range(S_TILES)]
-        out_dram = out.rearrange("b (p r) i -> p (b r) i", r=S_TILES)
-        products = {}
+        out_dram = out.rearrange("b (R p e) i -> p (b R) e i", R=S_PAIRS, e=2)
+        products, flips, sums = {}, {}, {}
+        gq = [keep.tile([P, 2, PASSES, HEADS_PER_PASS, HEAD_DIM], BF16, name="gq%d" % R) for R in range(S_PAIRS)]
 
-        def multiply_by_factors(j):
-            products[j] = scratch.tile([P, HEADS_PER_PASS, 2, ROPE], F32, name="products")
+        def copy_nope(R, c):
+            nc.scalar.copy(
+                out=gq[R][:, :, c].bitcast(F32)[:, :, :, 0 : NOPE // 2],
+                in_=raw[R][c][:].rearrange("p h e d -> p e h d").bitcast(F32)[:, :, :, 0 : NOPE // 2],
+            )
+
+        def multiply_by_factors(r, c):
+            products[r, c] = scratch.tile([P, HEADS_PER_PASS, 2, ROPE], F32, name="products")
             nc.vector.tensor_mul(
-                out=products[j][:],
-                in0=g_sb[j][:, :, NOPE:HEAD_DIM].unsqueeze(2).to_broadcast([P, HEADS_PER_PASS, 2, ROPE]),
-                in1=factors[:, j // PASSES].unsqueeze(1).to_broadcast([P, HEADS_PER_PASS, 2, ROPE]),
+                out=products[r, c][:],
+                in0=raw[r // 2][c][:, :, r % 2, NOPE:HEAD_DIM]
+                .unsqueeze(2)
+                .to_broadcast([P, HEADS_PER_PASS, 2, ROPE]),
+                in1=factors[:, r].unsqueeze(1).to_broadcast([P, HEADS_PER_PASS, 2, ROPE]),
             )
 
-        def add_products(j):
-            nc.vector.tensor_add(
-                out=g_sb[j][:, :, NOPE:HEAD_DIM].rearrange("p h (w j) -> p h w j", w=2),
-                in0=products[j][:, :, :, 0:HALF],
-                in1=products[j][:, :, :, HALF:ROPE],
+        def add_products(engine, r, c):
+            engine.tensor_add(
+                out=gq[r // 2][:, r % 2, c, :, NOPE:HEAD_DIM].rearrange("p h (w j) -> p h w j", w=2),
+                in0=products[r, c][:, :, :, 0:HALF],
+                in1=products[r, c][:, :, :, HALF:ROPE],
             )
 
-        def k_onto_partitions(block, words):
-            flipped = flip_banks.tile([P, 2, P], F32, name="flipped")
+        def flip_g(r, c):
+            if r not in flips:
+                flips[r] = flip_banks.tile([P, HALVES, P], F32, name="flipped")
+            words = gq[r // 2][:, r % 2, c].rearrange("p h d -> p (h d)").bitcast(F32)
             for u in range(2):
-                nc.tensor.transpose(flipped[:, u, :], block[:, u * P : (u + 1) * P], ident[:])
-            nc.scalar.copy(out=words, in_=flipped[:].rearrange("q u n -> q n u"))
+                nc.tensor.transpose(flips[r][:, 2 * c + u, :], words[:, u * P : (u + 1) * P], ident[:])
 
-        def quantise_g(j):
+        def gather_g(r, c0, c1):
+            nc.scalar.copy(
+                out=g_words[r][:, c0:c1], in_=flips[r][:, 2 * c0 : 2 * c1].rearrange("q (c u) n -> q c n u", u=2)
+            )
+
+        def flip_w(a):
+            flips["w", a] = flip_banks.tile([P, HALVES, P], F32, name="flipped")
+            words = w_sb[a][:].bitcast(F32)
+            for u in range(HALVES):
+                nc.tensor.transpose(flips["w", a][:, u, :], words[:, u * P : (u + 1) * P], ident[:])
+
+        def gather_w(a):
+            nc.scalar.copy(out=w_words[:, :, a], in_=flips["w", a][:].rearrange("q (c u) n -> q c n u", u=2))
+
+        def quantise_g(r, c0, c1):
             nc.vector.quantize_mx(
-                out=g_codes[j][:].bitcast(E5M2_X4),
-                scales=g_scales[j][:],
-                in_=g_words[j][:].rearrange("q n u -> q (n u)").bitcast(BF16),
+                out=g_codes[r][:, c0:c1].rearrange("q c n -> q (c n)").bitcast(E5M2_X4),
+                scales=g_scales[r][:, c0:c1].rearrange("q c n -> q (c n)"),
+                in_=g_words[r][:, c0:c1].rearrange("q c n u -> q (c n u)").bitcast(BF16),
             )
 
         def quantise_w(c):
             nc.vector.quantize_mx(
                 out=w_codes[c][:].bitcast(E4M3_X4),
                 scales=w_scales[c][:],
-                in_=w_words[c][:].rearrange("q a n u -> q (a n u)").bitcast(BF16),
+                in_=w_words[:, c].rearrange("q a n u -> q (a n u)").bitcast(BF16),
             )
 
         def multiply(r, c):
+            if c == 0:
+                sums[r] = sum_banks.tile([P, HID], F32, name="sums")
             nc.tensor.matmul_mx(
                 out=sums[r][:],
-                lhsT=g_codes[r * PASSES + c][:].bitcast(E5M2_X4),
-                lhsT_scale=g_scales[r * PASSES + c][:],
+                lhsT=g_codes[r][:, c].bitcast(E5M2_X4),
+                lhsT_scale=g_scales[r][:, c],
                 rhs=w_codes[c][:].bitcast(E4M3_X4),
                 rhs_scale=w_scales[c][:],
                 start=(c == 0),
@@ -130,33 +164,44 @@ def tile_gptossmlaattention_pb_s_kernel(tc, hidden_states, cos, sin, Wq, bq, gra
             )
 
         def store(r):
-            if r % 2 == 0:
-                nc.scalar.copy(out=result[r][:], in_=sums[r][:])
-            else:
-                nc.vector.tensor_copy(out=result[r][:], in_=sums[r][:])
-            nc.sync.dma_start(out=out_dram[:, r, :], in_=result[r][:])
+            parts = 2 if r == S_TILES - 1 else 1
+            for part in range(parts):
+                cols = slice(part * HID // parts, (part + 1) * HID // parts)
+                if (r + part) % 2 == 0:
+                    nc.scalar.copy(out=result[r][:, cols], in_=sums[r][:, cols])
+                else:
+                    nc.vector.tensor_copy(out=result[r][:, cols], in_=sums[r][:, cols])
+                nc.sync.dma_start(out=out_dram[:, r // 2, r % 2, cols], in_=result[r][:, cols])
 
-        def step_of_quantise_w(c):
-            return W_FIRST + 2 * c + 3
-
-        for step in range(UNITS + LAG):
-            if step < UNITS:
-                multiply_by_factors(step)
-            if 1 <= step <= UNITS:
-                add_products(step - 1)
-                k_onto_partitions(g_sb[step - 1][:].rearrange("p h d -> p (h d)").bitcast(F32), g_words[step - 1][:])
-            for b in range(2 * (step - W_FIRST), 2 * (step - W_FIRST) + 2):
-                if 0 <= b < W_BLOCKS:
-                    c, a = divmod(b, I_TILES)
-                    k_onto_partitions(w_sb[c][:, a, :].bitcast(F32), w_words[c][:, a])
-            if step >= LAG:
-                quantise_g(step - LAG)
-            for c in range(PASSES):
-                if step == step_of_quantise_w(c):
-                    quantise_w(c)
-            for c in range(PASSES):
-                for r in range(S_TILES):
-                    if max(r * PASSES + c + LAG, step_of_quantise_w(c)) == step:
-                        multiply(r, c)
+        units = [(2 * R + e, c) for R in range(S_PAIRS) for c in range(PASSES) for e in range(2)]
+        for j in range(4):
+            copy_nope(j // PASSES, j % PASSES)
+            for r, c in units[2 * j : 2 * j + 2]:
+                multiply_by_factors(r, c)
+                if (r, c) not in units[5:]:
+                    add_products(nc.gpsimd, r, c)
+            if j >= 1:
+                flip_w(j - 1)
+                gather_w(j - 1)
+            if j >= 2:
+                for r, c in units[2 * j - 4 : 2 * j - 2]:
+                    flip_g(r, c)
+        for r, c in units[5:]:
+            add_products(nc.vector, r, c)
+        flip_w(3)
+        gather_g(0, 0, 2)
+        gather_w(3)
+        gather_g(1, 0, 2)
+        for r, c in units[4:]:
+            flip_g(r, c)
+        for r in (2, 3):
+            gather_g(r, 0, 2)
+        quantise_g(0, 0, 2)
+        quantise_w(0)
+        quantise_w(1)
+        for r in (1, 2, 3):
+            quantise_g(r, 0, 2)
         for r in range(S_TILES):
+            for c in range(PASSES):
+                multiply(r, c)
             store(r)

@@ -36,7 +36,7 @@ def tile_gptossmlaattention_pb_s_kernel(tc, hidden_states, cos, sin, Wq, bq, gra
     nc = tc.nc
     with ExitStack() as ctx:
         keep = ctx.enter_context(tc.tile_pool(name="keep", bufs=1))
-        scratch = ctx.enter_context(tc.tile_pool(name="scratch", bufs=5))
+        scratch = ctx.enter_context(tc.tile_pool(name="scratch", bufs=8))
         flip_banks = ctx.enter_context(tc.psum_pool(name="flip_banks", bufs=5))
         sum_banks = ctx.enter_context(tc.psum_pool(name="sum_banks", bufs=3))
         ctx.enter_context(tc.manual_schedule())
@@ -47,39 +47,62 @@ def tile_gptossmlaattention_pb_s_kernel(tc, hidden_states, cos, sin, Wq, bq, gra
             [keep.tile([P, HEADS_PER_PASS, 2, HEAD_DIM], BF16, name="raw%d%d" % (R, c)) for c in range(PASSES)]
             for R in range(S_PAIRS)
         ]
-        w_sb = [keep.tile([P, K], BF16, name="w_sb%d" % a) for a in range(I_TILES)]
+        w_sb = [keep.tile([P, I_TILES, K_PASS], BF16, name="w_sb%d" % c) for c in range(PASSES)]
         g_dram = grad_out.rearrange("b (c h) (R p e) d -> R c p (b h) (e d)", c=PASSES, R=S_PAIRS, e=2)
-        w_dram = Wq.rearrange("(a p) k -> a p k", p=P)
+        w_dram = Wq.rearrange("(a p) (c k) -> c p a k", p=P, c=PASSES)
 
-        def load_g(R, c):
-            nc.sync.dma_start(out=raw[R][c][:].rearrange("p h e d -> p h (e d)"), in_=g_dram[R, c])
-
-        def load_w(a):
-            nc.sync.dma_start(out=w_sb[a][:], in_=w_dram[a])
-
-        def load_table(tile, table):
+        def load_g(R, c, heads=slice(0, HEADS_PER_PASS)):
             nc.sync.dma_start(
-                out=tile[:].rearrange("p (R e) j -> p R (e j)", e=2),
-                in_=table.rearrange("b (R p e) j -> p (b R) (e j)", R=S_PAIRS, e=2),
+                out=raw[R][c][:, heads].rearrange("p h e d -> p h (e d)"), in_=g_dram[R, c][:, heads]
             )
 
-        load_table(cos_sb, cos)
-        load_table(sin_sb, sin)
-        for j in range(4):
-            load_g(j // PASSES, j % PASSES)
-            load_w(j)
+        def weight_block(i):
+            c, half = divmod(i, 2)
+            return c, slice(half * I_TILES // 2, (half + 1) * I_TILES // 2)
+
+        def load_w(i):
+            c, tiles = weight_block(i)
+            nc.sync.dma_start(out=w_sb[c][:, tiles], in_=w_dram[c][:, tiles])
+
+        def load_tables(R):
+            for tile, table in ((cos_sb, cos), (sin_sb, sin)):
+                nc.sync.dma_start(
+                    out=tile[:, 2 * R : 2 * R + 2].rearrange("p e j -> p (e j)"),
+                    in_=table.rearrange("b (R p e) j -> R p (b e j)", R=S_PAIRS, e=2)[R],
+                )
+
+        first_heads = (slice(0, HEADS_PER_PASS // 2), slice(HEADS_PER_PASS // 2, HEADS_PER_PASS))
+        load_tables(0)
+        for heads in first_heads:
+            load_g(0, 0, heads)
+        load_w(0)
+        load_g(0, 1)
+        load_tables(1)
+        load_g(1, 0)
+        load_w(1)
+        load_g(1, 1)
+        load_w(2)
+        load_w(3)
 
         ident = keep.tile([P, P], F32, name="ident")
         make_identity(nc, ident[:])
+
+        first = keep.tile([P, 1], F32, name="first")
+        nc.scalar.copy(out=first[:], in_=ident[:, 0:1])
 
         plus = keep.tile([P, P], BF16, name="plus")
         minus = keep.tile([P, P], BF16, name="minus")
         nc.vector.tensor_copy(out=plus[:], in_=ident[:])
         nc.vector.tensor_scalar_mul(out=minus[:], in0=ident[:], scalar1=-1.0)
-        factors = sum_banks.tile([P, S_TILES, 2, ROPE], F32, name="sums")
-        for w, half, sign, table in ((0, 0, plus, cos_sb), (0, 1, plus, sin_sb), (1, 0, minus, sin_sb), (1, 1, plus, cos_sb)):
-            part = slice(half * HALF, (half + 1) * HALF)
-            nc.tensor.matmul(factors[:, :, w, part], lhsT=sign[:], rhs=table[:, :, part], start=True, stop=True)
+        factors = [sum_banks.tile([P, 2, 2, ROPE], F32, name="sums") for R in range(S_PAIRS)]
+
+        def make_factors(R):
+            r = slice(2 * R, 2 * R + 2)
+            for w, half, sign, table in ((0, 0, plus, cos_sb), (0, 1, plus, sin_sb), (1, 0, minus, sin_sb), (1, 1, plus, cos_sb)):
+                part = slice(half * HALF, (half + 1) * HALF)
+                nc.tensor.matmul(factors[R][:, :, w, part], lhsT=sign[:], rhs=table[:, r, part], start=True, stop=True)
+
+        make_factors(0)
 
         g_words = [keep.tile([P, PASSES, P, 2], F32, name="g_words%d" % r, align_bytes=64) for r in range(S_TILES)]
         g_codes = [keep.tile([P, PASSES, P], U32, name="g_codes%d" % r, align_bytes=64) for r in range(S_TILES)]
@@ -98,14 +121,14 @@ def tile_gptossmlaattention_pb_s_kernel(tc, hidden_states, cos, sin, Wq, bq, gra
                 in_=raw[R][c][:].rearrange("p h e d -> p e h d").bitcast(F32)[:, :, :, 0 : NOPE // 2],
             )
 
-        def multiply_by_factors(r, c):
-            products[r, c] = scratch.tile([P, HEADS_PER_PASS, 2, ROPE], F32, name="products")
+        def multiply_by_factors(r, c, heads=slice(0, HEADS_PER_PASS)):
+            if (r, c) not in products:
+                products[r, c] = scratch.tile([P, HEADS_PER_PASS, 2, ROPE], F32, name="products")
+            shape = [P, heads.stop - heads.start, 2, ROPE]
             nc.vector.tensor_mul(
-                out=products[r, c][:],
-                in0=raw[r // 2][c][:, :, r % 2, NOPE:HEAD_DIM]
-                .unsqueeze(2)
-                .to_broadcast([P, HEADS_PER_PASS, 2, ROPE]),
-                in1=factors[:, r].unsqueeze(1).to_broadcast([P, HEADS_PER_PASS, 2, ROPE]),
+                out=products[r, c][:, heads],
+                in0=raw[r // 2][c][:, heads, r % 2, NOPE:HEAD_DIM].unsqueeze(2).to_broadcast(shape),
+                in1=factors[r // 2][:, r % 2].unsqueeze(1).to_broadcast(shape),
             )
 
         def add_products(engine, r, c):
@@ -127,14 +150,16 @@ def tile_gptossmlaattention_pb_s_kernel(tc, hidden_states, cos, sin, Wq, bq, gra
                 out=g_words[r][:, c0:c1], in_=flips[r][:, 2 * c0 : 2 * c1].rearrange("q (c u) n -> q c n u", u=2)
             )
 
-        def flip_w(a):
-            flips["w", a] = flip_banks.tile([P, HALVES, P], F32, name="flipped")
-            words = w_sb[a][:].bitcast(F32)
+        def flip_w(i):
+            c, tiles = weight_block(i)
+            flips["w", i] = flip_banks.tile([P, HALVES, P], F32, name="flipped")
+            words = w_sb[c][:, tiles].rearrange("p a k -> p (a k)").bitcast(F32)
             for u in range(HALVES):
-                nc.tensor.transpose(flips["w", a][:, u, :], words[:, u * P : (u + 1) * P], ident[:])
+                nc.tensor.transpose(flips["w", i][:, u, :], words[:, u * P : (u + 1) * P], ident[:])
 
-        def gather_w(a):
-            nc.scalar.copy(out=w_words[:, :, a], in_=flips["w", a][:].rearrange("q (c u) n -> q c n u", u=2))
+        def gather_w(i):
+            c, tiles = weight_block(i)
+            nc.scalar.copy(out=w_words[:, c, tiles], in_=flips["w", i][:].rearrange("q (a u) n -> q a n u", u=2))
 
         def quantise_g(r, c0, c1):
             nc.vector.quantize_mx(
@@ -174,30 +199,39 @@ def tile_gptossmlaattention_pb_s_kernel(tc, hidden_states, cos, sin, Wq, bq, gra
                 nc.sync.dma_start(out=out_dram[:, r // 2, r % 2, cols], in_=result[r][:, cols])
 
         units = [(2 * R + e, c) for R in range(S_PAIRS) for c in range(PASSES) for e in range(2)]
-        for j in range(4):
-            copy_nope(j // PASSES, j % PASSES)
-            for r, c in units[2 * j : 2 * j + 2]:
-                multiply_by_factors(r, c)
-                if (r, c) not in units[5:]:
-                    add_products(nc.gpsimd, r, c)
-            if j >= 1:
-                flip_w(j - 1)
-                gather_w(j - 1)
-            if j >= 2:
-                for r, c in units[2 * j - 4 : 2 * j - 2]:
-                    flip_g(r, c)
-        for r, c in units[5:]:
-            add_products(nc.vector, r, c)
-        flip_w(3)
+        on_vector = units[5:]
+        copy_nope(0, 0)
+        for heads in first_heads:
+            for r, c in units[0:2]:
+                multiply_by_factors(r, c, heads)
+        copy_nope(0, 1)
+        flip_w(0)
+        gather_w(0)
+        make_factors(1)
+        for r, c in units[2:]:
+            multiply_by_factors(r, c)
+        copy_nope(1, 0)
+        copy_nope(1, 1)
+        for r, c in units:
+            add_products(nc.vector if (r, c) in on_vector else nc.gpsimd, r, c)
+        flip_g(*units[0])
+        flip_w(1)
+        gather_w(1)
+        flip_g(*units[1])
+        flip_g(*units[2])
         gather_g(0, 0, 2)
+        flip_w(2)
+        gather_w(2)
+        flip_w(3)
         gather_w(3)
+        flip_g(*units[3])
         gather_g(1, 0, 2)
         for r, c in units[4:]:
             flip_g(r, c)
         for r in (2, 3):
             gather_g(r, 0, 2)
-        quantise_g(0, 0, 2)
         quantise_w(0)
+        quantise_g(0, 0, 2)
         quantise_w(1)
         for r in (1, 2, 3):
             quantise_g(r, 0, 2)

@@ -102,6 +102,13 @@ def tile_gptossmlaattention_pb_s_kernel(tc, hidden_states, cos, sin, Wq, bq, gra
                 part = slice(half * HALF, (half + 1) * HALF)
                 nc.tensor.matmul(factors[R][:, :, w, part], lhsT=sign[:], rhs=table[:, r, part], start=True, stop=True)
 
+        pulse_bank = sum_banks.tile([P, HID], F32, name="sums")
+
+        def pulse():
+            nc.tensor.matmul(pulse_bank[:, 0:P], lhsT=ident[:], rhs=ident[:], start=True, stop=True)
+
+        pulse()
+        pulse()
         make_factors(0)
 
         g_words = [keep.tile([P, PASSES, P, 2], F32, name="g_words%d" % r, align_bytes=64) for r in range(S_TILES)]
@@ -206,8 +213,10 @@ def tile_gptossmlaattention_pb_s_kernel(tc, hidden_states, cos, sin, Wq, bq, gra
                 multiply_by_factors(r, c, heads)
         copy_nope(0, 1)
         flip_w(0)
+        pulse()
         gather_w(0)
         make_factors(1)
+        pulse()
         for r, c in units[2:]:
             multiply_by_factors(r, c)
         copy_nope(1, 0)
@@ -216,18 +225,22 @@ def tile_gptossmlaattention_pb_s_kernel(tc, hidden_states, cos, sin, Wq, bq, gra
             add_products(nc.vector if (r, c) in on_vector else nc.gpsimd, r, c)
         flip_g(*units[0])
         flip_w(1)
+        pulse()
         gather_w(1)
         flip_g(*units[1])
         flip_g(*units[2])
         gather_g(0, 0, 2)
         flip_w(2)
+        pulse()
         gather_w(2)
         flip_w(3)
+        pulse()
         gather_w(3)
         flip_g(*units[3])
         gather_g(1, 0, 2)
         for r, c in units[4:]:
             flip_g(r, c)
+        pulse()
         for r in (2, 3):
             gather_g(r, 0, 2)
         quantise_w(0)

@@ -48,7 +48,7 @@ def tile_gptossmlaattention_pb_s_kernel(tc, hidden_states, cos, sin, Wq, bq, gra
             for R in range(S_PAIRS)
         ]
         w_sb = [keep.tile([P, I_TILES, K_PASS], BF16, name="w_sb%d" % c) for c in range(PASSES)]
-        g_dram = grad_out.rearrange("b (c h) (R p e) d -> R c p (b h) (e d)", c=PASSES, R=S_PAIRS, e=2)
+        g_dram = grad_out.rearrange("b (c h) (p R e) d -> R c p (b h) (e d)", c=PASSES, R=S_PAIRS, e=2)
         w_dram = Wq.rearrange("(a p) (c k) -> c p a k", p=P, c=PASSES)
 
         def load_g(R, c, heads=slice(0, HEADS_PER_PASS)):
@@ -64,24 +64,23 @@ def tile_gptossmlaattention_pb_s_kernel(tc, hidden_states, cos, sin, Wq, bq, gra
             c, tiles = weight_block(i)
             nc.sync.dma_start(out=w_sb[c][:, tiles], in_=w_dram[c][:, tiles])
 
-        def load_tables(R):
-            for tile, table in ((cos_sb, cos), (sin_sb, sin)):
-                nc.sync.dma_start(
-                    out=tile[:, 2 * R : 2 * R + 2].rearrange("p e j -> p (e j)"),
-                    in_=table.rearrange("b (R p e) j -> R p (b e j)", R=S_PAIRS, e=2)[R],
-                )
+        def load_table(tile, table):
+            nc.sync.dma_start(
+                out=tile[:].rearrange("p r j -> p (r j)"),
+                in_=table.rearrange("b (p r) j -> p (b r j)", r=S_TILES),
+            )
 
         first_heads = (slice(0, HEADS_PER_PASS // 2), slice(HEADS_PER_PASS // 2, HEADS_PER_PASS))
-        load_tables(0)
+        load_table(cos_sb, cos)
+        load_table(sin_sb, sin)
         for heads in first_heads:
             load_g(0, 0, heads)
         load_w(0)
         load_g(0, 1)
-        load_tables(1)
-        load_g(1, 0)
         load_w(1)
-        load_g(1, 1)
+        load_g(1, 0)
         load_w(2)
+        load_g(1, 1)
         load_w(3)
 
         ident = keep.tile([P, P], F32, name="ident")
@@ -118,7 +117,7 @@ def tile_gptossmlaattention_pb_s_kernel(tc, hidden_states, cos, sin, Wq, bq, gra
         w_codes = [keep.tile([P, HID], U32, name="w_codes%d" % c, align_bytes=64) for c in range(PASSES)]
         w_scales = [keep.tile([P, HID], U8, name="w_scales%d" % c, align_bytes=64) for c in range(PASSES)]
         result = [keep.tile([P, HID], F32, name="result%d" % r) for r in range(S_TILES)]
-        out_dram = out.rearrange("b (R p e) i -> p (b R) e i", R=S_PAIRS, e=2)
+        out_dram = out.rearrange("b (p R e) i -> p (b R) e i", R=S_PAIRS, e=2)
         products, flips, sums = {}, {}, {}
         gq = [keep.tile([P, 2, PASSES, HEADS_PER_PASS, HEAD_DIM], BF16, name="gq%d" % R) for R in range(S_PAIRS)]
 
@@ -219,20 +218,20 @@ def tile_gptossmlaattention_pb_s_kernel(tc, hidden_states, cos, sin, Wq, bq, gra
         pulse()
         for r, c in units[2:]:
             multiply_by_factors(r, c)
-        copy_nope(1, 0)
-        copy_nope(1, 1)
         for r, c in units:
             add_products(nc.vector if (r, c) in on_vector else nc.gpsimd, r, c)
-        flip_g(*units[0])
         flip_w(1)
         pulse()
         gather_w(1)
+        copy_nope(1, 0)
+        copy_nope(1, 1)
+        flip_g(*units[0])
         flip_g(*units[1])
-        flip_g(*units[2])
-        gather_g(0, 0, 2)
         flip_w(2)
         pulse()
         gather_w(2)
+        flip_g(*units[2])
+        gather_g(0, 0, 2)
         flip_w(3)
         pulse()
         gather_w(3)

@@ -106,9 +106,9 @@ def tile_gptossmlaattention_pb_s_kernel(tc, hidden_states, cos, sin, Wq, bq, gra
         def pulse():
             nc.tensor.matmul(pulse_bank[:, 0:P], lhsT=ident[:], rhs=ident[:], start=True, stop=True)
 
-        pulse()
-        pulse()
         make_factors(0)
+        pulse()
+        pulse()
 
         g_words = [keep.tile([P, PASSES, P, 2], F32, name="g_words%d" % r, align_bytes=64) for r in range(S_TILES)]
         g_codes = [keep.tile([P, PASSES, P], U32, name="g_codes%d" % r, align_bytes=64) for r in range(S_TILES)]
@@ -212,7 +212,6 @@ def tile_gptossmlaattention_pb_s_kernel(tc, hidden_states, cos, sin, Wq, bq, gra
                 multiply_by_factors(r, c, heads)
         copy_nope(0, 1)
         flip_w(0)
-        pulse()
         gather_w(0)
         make_factors(1)
         pulse()
@@ -236,6 +235,7 @@ def tile_gptossmlaattention_pb_s_kernel(tc, hidden_states, cos, sin, Wq, bq, gra
         pulse()
         gather_w(3)
         flip_g(*units[3])
+        pulse()
         gather_g(1, 0, 2)
         for r, c in units[4:]:
             flip_g(r, c)

@@ -75,12 +75,12 @@ def tile_gptossmlaattention_pb_s_kernel(tc, hidden_states, cos, sin, Wq, bq, gra
         load_table(sin_sb, sin)
         for heads in first_heads:
             load_g(0, 0, heads)
-        load_w(0)
         load_g(0, 1)
-        load_w(1)
+        load_w(0)
         load_g(1, 0)
-        load_w(2)
+        load_w(1)
         load_g(1, 1)
+        load_w(2)
         load_w(3)
 
         ident = keep.tile([P, P], F32, name="ident")
@@ -207,8 +207,8 @@ def tile_gptossmlaattention_pb_s_kernel(tc, hidden_states, cos, sin, Wq, bq, gra
         units = [(2 * R + e, c) for R in range(S_PAIRS) for c in range(PASSES) for e in range(2)]
         on_vector = units[5:]
         copy_nope(0, 0)
-        for heads in first_heads:
-            for r, c in units[0:2]:
+        for r, c in units[0:2]:
+            for heads in first_heads:
                 multiply_by_factors(r, c, heads)
         copy_nope(0, 1)
         flip_w(0)
@@ -221,8 +221,8 @@ def tile_gptossmlaattention_pb_s_kernel(tc, hidden_states, cos, sin, Wq, bq, gra
             add_products(nc.vector if (r, c) in on_vector else nc.gpsimd, r, c)
         flip_w(1)
         pulse()
-        gather_w(1)
         copy_nope(1, 0)
+        gather_w(1)
         copy_nope(1, 1)
         flip_g(*units[0])
         flip_g(*units[1])

@@ -205,7 +205,7 @@ def tile_gptossmlaattention_pb_s_kernel(tc, hidden_states, cos, sin, Wq, bq, gra
                 nc.sync.dma_start(out=out_dram[:, r // 2, r % 2, cols], in_=result[r][:, cols])
 
         units = [(2 * R + e, c) for R in range(S_PAIRS) for c in range(PASSES) for e in range(2)]
-        on_vector = units[5:]
+        on_vector = units[6:]
         copy_nope(0, 0)
         for r, c in units[0:2]:
             for heads in first_heads:
@@ -226,22 +226,24 @@ def tile_gptossmlaattention_pb_s_kernel(tc, hidden_states, cos, sin, Wq, bq, gra
         copy_nope(1, 1)
         flip_g(*units[0])
         flip_g(*units[1])
+        flip_g(*units[2])
+        gather_g(0, 0, 2)
         flip_w(2)
         pulse()
         gather_w(2)
-        flip_g(*units[2])
-        gather_g(0, 0, 2)
         flip_w(3)
         pulse()
         gather_w(3)
         flip_g(*units[3])
         pulse()
         gather_g(1, 0, 2)
-        for r, c in units[4:]:
+        flip_g(*units[4])
+        for r, c in on_vector:
             flip_g(r, c)
+        gather_g(2, 0, 2)
         pulse()
-        for r in (2, 3):
-            gather_g(r, 0, 2)
+        flip_g(*units[5])
+        gather_g(3, 0, 2)
         quantise_w(0)
         quantise_g(0, 0, 2)
         quantise_w(1)

from contextlib import ExitStack

import concourse.mybir as mybir
from concourse.masks import make_identity

BF16 = mybir.dt.bfloat16
F32 = mybir.dt.float32
U32 = mybir.dt.uint32
U8 = mybir.dt.uint8
E4M3_X4 = mybir.dt.float8_e4m3fn_x4
E5M2_X4 = mybir.dt.float8_e5m2_x4

P = 128
SEQ = 512
HID = 512
HEADS = 8
HEAD_DIM = 128
NOPE = 64
ROPE = 64
HALF = ROPE // 2
K = HEADS * HEAD_DIM
K_PASS = 4 * P
PASSES = K // K_PASS
S_TILES = SEQ // P
I_TILES = HID // P
HEADS_PER_PASS = K_PASS // HEAD_DIM
UNITS = S_TILES * PASSES
HALVES = 2 * PASSES
S_PAIRS = S_TILES // 2

FLOPS = 2 * SEQ * HID * K
BYTES = 2 * (2 * SEQ * ROPE + HID * K + SEQ * K) + 4 * SEQ * HID


def tile_gptossmlaattention_pb_s_kernel(tc, hidden_states, cos, sin, Wq, bq, grad_out, out):
    nc = tc.nc
    with ExitStack() as ctx:
        keep = ctx.enter_context(tc.tile_pool(name="keep", bufs=1))
        scratch = ctx.enter_context(tc.tile_pool(name="scratch", bufs=8))
        flip_banks = ctx.enter_context(tc.psum_pool(name="flip_banks", bufs=5))
        sum_banks = ctx.enter_context(tc.psum_pool(name="sum_banks", bufs=3))
        ctx.enter_context(tc.manual_schedule())

        cos_sb = keep.tile([P, S_TILES, ROPE], BF16, name="cos_sb")
        sin_sb = keep.tile([P, S_TILES, ROPE], BF16, name="sin_sb")
        raw = [
            [keep.tile([P, HEADS_PER_PASS, 2, HEAD_DIM], BF16, name="raw%d%d" % (R, c)) for c in range(PASSES)]
            for R in range(S_PAIRS)
        ]
        w_sb = [keep.tile([P, I_TILES, K_PASS], BF16, name="w_sb%d" % c) for c in range(PASSES)]
        g_dram = grad_out.rearrange("b (c h) (p R e) d -> R c p (b h) (e d)", c=PASSES, R=S_PAIRS, e=2)
        w_dram = Wq.rearrange("(a p) (c k) -> c p a k", p=P, c=PASSES)

        def load_g(R, c, heads=slice(0, HEADS_PER_PASS)):
            nc.sync.dma_start(
                out=raw[R][c][:, heads].rearrange("p h e d -> p h (e d)"), in_=g_dram[R, c][:, heads]
            )

        def weight_block(i):
            c, half = divmod(i, 2)
            return c, slice(half * I_TILES // 2, (half + 1) * I_TILES // 2)

        def load_w(i):
            c, tiles = weight_block(i)
            nc.sync.dma_start(out=w_sb[c][:, tiles], in_=w_dram[c][:, tiles])

        def load_table(tile, table):
            nc.sync.dma_start(
                out=tile[:].rearrange("p r j -> p (r j)"),
                in_=table.rearrange("b (p r) j -> p (b r j)", r=S_TILES),
            )

        first_heads = (slice(0, HEADS_PER_PASS // 2), slice(HEADS_PER_PASS // 2, HEADS_PER_PASS))
        load_table(cos_sb, cos)
        load_table(sin_sb, sin)
        for heads in first_heads:
            load_g(0, 0, heads)
        load_g(0, 1)
        load_w(0)
        load_g(1, 0)
        load_w(1)
        load_g(1, 1)
        load_w(2)
        load_w(3)

        ident = keep.tile([P, P], F32, name="ident")
        make_identity(nc, ident[:])

        first = keep.tile([P, 1], F32, name="first")
        nc.scalar.copy(out=first[:], in_=ident[:, 0:1])

        plus = keep.tile([P, P], BF16, name="plus")
        minus = keep.tile([P, P], BF16, name="minus")
        nc.vector.tensor_copy(out=plus[:], in_=ident[:])
        nc.vector.tensor_scalar_mul(out=minus[:], in0=ident[:], scalar1=-1.0)
        factors = [sum_banks.tile([P, 2, 2, ROPE], F32, name="sums") for R in range(S_PAIRS)]

        def make_factors(R):
            r = slice(2 * R, 2 * R + 2)
            for w, half, sign, table in ((0, 0, plus, cos_sb), (0, 1, plus, sin_sb), (1, 0, minus, sin_sb), (1, 1, plus, cos_sb)):
                part = slice(half * HALF, (half + 1) * HALF)
                nc.tensor.matmul(factors[R][:, :, w, part], lhsT=sign[:], rhs=table[:, r, part], start=True, stop=True)

        pulse_bank = sum_banks.tile([P, HID], F32, name="sums")

        def pulse():
            nc.tensor.matmul(pulse_bank[:, 0:P], lhsT=ident[:], rhs=ident[:], start=True, stop=True)

        make_factors(0)
        pulse()
        pulse()

        g_words = [keep.tile([P, PASSES, P, 2], F32, name="g_words%d" % r, align_bytes=64) for r in range(S_TILES)]
        g_codes = [keep.tile([P, PASSES, P], U32, name="g_codes%d" % r, align_bytes=64) for r in range(S_TILES)]
        g_scales = [keep.tile([P, PASSES, P], U8, name="g_scales%d" % r, align_bytes=64) for r in range(S_TILES)]
        w_words = keep.tile([P, PASSES, I_TILES, P, 2], F32, name="w_words", align_bytes=64)
        w_codes = [keep.tile([P, HID], U32, name="w_codes%d" % c, align_bytes=64) for c in range(PASSES)]
        w_scales = [keep.tile([P, HID], U8, name="w_scales%d" % c, align_bytes=64) for c in range(PASSES)]
        result = [keep.tile([P, HID], F32, name="result%d" % r) for r in range(S_TILES)]
        out_dram = out.rearrange("b (p R e) i -> p (b R) e i", R=S_PAIRS, e=2)
        products, flips, sums = {}, {}, {}
        gq = [keep.tile([P, 2, PASSES, HEADS_PER_PASS, HEAD_DIM], BF16, name="gq%d" % R) for R in range(S_PAIRS)]

        def copy_nope(R, c):
            nc.scalar.copy(
                out=gq[R][:, :, c].bitcast(F32)[:, :, :, 0 : NOPE // 2],
                in_=raw[R][c][:].rearrange("p h e d -> p e h d").bitcast(F32)[:, :, :, 0 : NOPE // 2],
            )

        def multiply_by_factors(r, c, heads=slice(0, HEADS_PER_PASS)):
            if (r, c) not in products:
                products[r, c] = scratch.tile([P, HEADS_PER_PASS, 2, ROPE], F32, name="products")
            shape = [P, heads.stop - heads.start, 2, ROPE]
            nc.vector.tensor_mul(
                out=products[r, c][:, heads],
                in0=raw[r // 2][c][:, heads, r % 2, NOPE:HEAD_DIM].unsqueeze(2).to_broadcast(shape),
                in1=factors[r // 2][:, r % 2].unsqueeze(1).to_broadcast(shape),
            )

        def add_products(engine, r, c):
            engine.tensor_add(
                out=gq[r // 2][:, r % 2, c, :, NOPE:HEAD_DIM].rearrange("p h (w j) -> p h w j", w=2),
                in0=products[r, c][:, :, :, 0:HALF],
                in1=products[r, c][:, :, :, HALF:ROPE],
            )

        def flip_g(r, c):
            if r not in flips:
                flips[r] = flip_banks.tile([P, HALVES, P], F32, name="flipped")
            words = gq[r // 2][:, r % 2, c].rearrange("p h d -> p (h d)").bitcast(F32)
            for u in range(2):
                nc.tensor.transpose(flips[r][:, 2 * c + u, :], words[:, u * P : (u + 1) * P], ident[:])

        def gather_g(r, c0, c1):
            nc.scalar.copy(
                out=g_words[r][:, c0:c1], in_=flips[r][:, 2 * c0 : 2 * c1].rearrange("q (c u) n -> q c n u", u=2)
            )

        def flip_w(i):
            c, tiles = weight_block(i)
            flips["w", i] = flip_banks.tile([P, HALVES, P], F32, name="flipped")
            words = w_sb[c][:, tiles].rearrange("p a k -> p (a k)").bitcast(F32)
            for u in range(HALVES):
                nc.tensor.transpose(flips["w", i][:, u, :], words[:, u * P : (u + 1) * P], ident[:])

        def gather_w(i):
            c, tiles = weight_block(i)
            nc.scalar.copy(out=w_words[:, c, tiles], in_=flips["w", i][:].rearrange("q (a u) n -> q a n u", u=2))

        def quantise_g(r, c0, c1):
            nc.vector.quantize_mx(
                out=g_codes[r][:, c0:c1].rearrange("q c n -> q (c n)").bitcast(E5M2_X4),
                scales=g_scales[r][:, c0:c1].rearrange("q c n -> q (c n)"),
                in_=g_words[r][:, c0:c1].rearrange("q c n u -> q (c n u)").bitcast(BF16),
            )

        def quantise_w(c):
            nc.vector.quantize_mx(
                out=w_codes[c][:].bitcast(E4M3_X4),
                scales=w_scales[c][:],
                in_=w_words[:, c].rearrange("q a n u -> q (a n u)").bitcast(BF16),
            )

        def multiply(r, c):
            if c == 0:
                sums[r] = sum_banks.tile([P, HID], F32, name="sums")
            nc.tensor.matmul_mx(
                out=sums[r][:],
                lhsT=g_codes[r][:, c].bitcast(E5M2_X4),
                lhsT_scale=g_scales[r][:, c],
                rhs=w_codes[c][:].bitcast(E4M3_X4),
                rhs_scale=w_scales[c][:],
                start=(c == 0),
                stop=(c == PASSES - 1),
            )

        def store(r):
            parts = 2 if r == S_TILES - 1 else 1
            for part in range(parts):
                cols = slice(part * HID // parts, (part + 1) * HID // parts)
                if (r + part) % 2 == 0:
                    nc.scalar.copy(out=result[r][:, cols], in_=sums[r][:, cols])
                else:
                    nc.vector.tensor_copy(out=result[r][:, cols], in_=sums[r][:, cols])
                nc.sync.dma_start(out=out_dram[:, r // 2, r % 2, cols], in_=result[r][:, cols])

        units = [(2 * R + e, c) for R in range(S_PAIRS) for c in range(PASSES) for e in range(2)]
        on_vector = units[6:]
        copy_nope(0, 0)
        for r, c in units[0:2]:
            for heads in first_heads:
                multiply_by_factors(r, c, heads)
        copy_nope(0, 1)
        flip_w(0)
        gather_w(0)
        make_factors(1)
        pulse()
        for r, c in units[2:]:
            multiply_by_factors(r, c)
        for r, c in units:
            add_products(nc.vector if (r, c) in on_vector else nc.gpsimd, r, c)
        flip_w(1)
        pulse()
        copy_nope(1, 0)
        gather_w(1)
        copy_nope(1, 1)
        flip_g(*units[0])
        flip_g(*units[1])
        flip_g(*units[2])
        gather_g(0, 0, 2)
        flip_w(2)
        pulse()
        gather_w(2)
        flip_w(3)
        pulse()
        gather_w(3)
        flip_g(*units[3])
        pulse()
        gather_g(1, 0, 2)
        flip_g(*units[4])
        for r, c in on_vector:
            flip_g(r, c)
        gather_g(2, 0, 2)
        pulse()
        flip_g(*units[5])
        gather_g(3, 0, 2)
        quantise_w(0)
        quantise_g(0, 0, 2)
        quantise_w(1)
        for r in (1, 2, 3):
            quantise_g(r, 0, 2)
        for r in range(S_TILES):
            for c in range(PASSES):
                multiply(r, c)
            store(r)
